import numpy as np
import ml_dtypes


def mxq(x, axis, fmt="e4m3"):
    dtype, down = {"e4m3": (ml_dtypes.float8_e4m3fn, 7), "e5m2": (ml_dtypes.float8_e5m2, 14)}[fmt]
    v = np.moveaxis(np.asarray(x, np.float32).astype(ml_dtypes.bfloat16).astype(np.float64), axis, -1)
    blocks = v.reshape(v.shape[:-1] + (-1, 32))
    amax = np.abs(blocks).max(-1, keepdims=True)
    byte = np.maximum(np.where(amax > 0, np.frexp(amax)[1] - 1 + 127, 0) - down, 1)
    scale = np.exp2(byte - 127.0)
    codes = (blocks / scale).astype(np.float32).astype(dtype).astype(np.float64)
    return np.moveaxis((codes * scale).reshape(v.shape), -1, axis)


WIDE = False


def mx_kscale(k):
    if not WIDE:
        return np.ones(k)
    levels = np.array([20, -20, 10, -10, 0])
    a = np.random.permutation(np.resize(levels, k // 512 * 4)).reshape(k // 512, 4)
    idx = np.arange(k)
    return np.exp2(a[idx // 512, idx % 128 // 32])


BF16 = ml_dtypes.bfloat16


def bf(x):
    return np.asarray(x, np.float32).astype(BF16)


def f64(x):
    return np.asarray(x).astype(np.float64)


B, IN, OUT = 8192, 512, 512


def setup_inputs():
    u = mx_kscale(OUT)
    x = np.random.standard_normal((B, IN))
    w = np.random.standard_normal((OUT, IN)) / np.sqrt(IN) / u[:, None]
    b = np.random.standard_normal(OUT) * 0.5
    pg = np.random.standard_normal((OUT, IN)) / np.sqrt(IN) / u[:, None]
    pb = np.random.standard_normal(OUT) * 0.5
    lr = np.random.uniform(0.1, 1.0, B)
    g = np.random.standard_normal((B, OUT)) * np.exp2(np.random.randint(-12, 1, (B, 1))) * 16.0 * u
    return {"input_data": bf(x), "weight": bf(w), "bias": bf(b), "prev_grad": bf(pg),
            "prev_bias_grad": bf(pb), "lr_samples": bf(lr), "grad_out": bf(g)}


def reference(input_data, weight, bias, prev_grad, prev_bias_grad, lr_samples, grad_out):
    gq = mxq(f64(grad_out), 1, "e5m2")
    a = gq @ mxq(f64(weight), 0, "e4m3")
    p = gq @ mxq(f64(prev_grad), 0, "e4m3")
    return a - f64(lr_samples)[:, None] * p

@@ -1,0 +1,233 @@
+from contextlib import ExitStack
+
+import concourse.mybir as mybir
+from concourse.masks import make_identity
+
+F32 = mybir.dt.float32
+BF16 = mybir.dt.bfloat16
+U32 = mybir.dt.uint32
+U8 = mybir.dt.uint8
+E4X4 = mybir.dt.float8_e4m3fn_x4
+E5X4 = mybir.dt.float8_e5m2_x4
+MULT = mybir.AluOpType.mult
+ADD = mybir.AluOpType.add
+
+P = 128
+B, K, N = 8192, 512, 512
+NT = B // P
+FLOPS = 2 * 2 * B * K * N
+BYTES = B * K * 2 + 2 * K * N * 2 + B * 2 + B * N * 4
+
+G_CHUNKS = [2, 2, 4, 8, 16, 16, 16]
+S_CHUNKS = [4] * 13 + [2, 2, 2, 2, 1, 1, 1, 1]
+STAGE_BUFS = 8
+ASB_BUFS = 4
+GRP_BUFS = 4
+CV = 336
+
+
+def front_groups():
+    groups = [(1, 1, 0, None), (2, 2, 2, 1), (4, 4, 4, 2)]
+    for j in range(2, 8):
+        groups.append((4 * j, 4, 8 * j - 2, 2))
+    return groups
+
+
+def tile_optimizedlinear_t_kernel(
+    tc, input_data, weight, bias, prev_grad, prev_bias_grad, lr_samples, grad_out, out
+):
+    nc = tc.nc
+    g_rows = grad_out.rearrange("(p n) k -> p (n k)", n=NT)
+    out_rows = out.rearrange("(p n) i -> p (n i)", n=NT)
+    lr_rows = lr_samples.rearrange("(p n) -> p n", n=NT)
+
+    with ExitStack() as ctx:
+        keep = ctx.enter_context(tc.tile_pool(name="keep", bufs=1))
+        ring = ctx.enter_context(tc.tile_pool(name="ring", bufs=1))
+        psum = ctx.enter_context(tc.psum_pool(name="psum", bufs=1))
+        ctx.enter_context(tc.manual_schedule())
+
+        ident = keep.tile([P, P], F32, name="ident")
+        make_identity(nc, ident[:])
+
+        raw = {}
+        for nm in ("w", "pg"):
+            raw[nm] = keep.tile([P, 4, N], BF16, name="raw_" + nm)
+        lrb = keep.tile([P, NT], BF16, name="lrb")
+        g_tiles = []
+        chunk_of = []
+        t0 = 0
+        for ci, sz in enumerate(G_CHUNKS):
+            g_tiles.append(keep.tile([P, sz * K], BF16, name="g%d" % ci))
+            for j in range(sz):
+                chunk_of.append((ci, j))
+            t0 += sz
+
+        def load_w(nm, src):
+            nc.sync.dma_start(
+                out=raw[nm][:].rearrange("p (u e) c -> p u (e c)", u=2),
+                in_=src.rearrange("(u q e) c -> q u (e c)", u=2, e=2),
+            )
+
+        def load_g(ci):
+            first = sum(G_CHUNKS[:ci])
+            nc.sync.dma_start(out=g_tiles[ci][:], in_=g_rows[:, first * K : (first + G_CHUNKS[ci]) * K])
+
+        load_w("w", weight)
+        load_g(0)
+        load_w("pg", prev_grad)
+        nc.sync.dma_start(out=lrb[:], in_=lr_rows)
+        for ci in range(1, len(G_CHUNKS)):
+            load_g(ci)
+
+        free_banks = list(range(8))
+        head = [0]
+        serial = [0]
+
+        def new_bank():
+            k = free_banks[head[0]]
+            head[0] += 1
+            serial[0] += 1
+            return k, psum.tile([P, 512], F32, name="ps%d" % serial[0], tag="bank%d" % k)
+
+        wgrp, wcodes, wscales = {}, {}, {}
+
+        def regroup_w(nm):
+            wgrp[nm] = keep.tile([P, N, 4], BF16, name="grp_" + nm, align_bytes=64)
+            nc.vector.tensor_copy(
+                out=wgrp[nm][:, 0:CV, :].rearrange("p (c i) t -> p c t i", i=4),
+                in_=raw[nm][:, :, 0:CV].rearrange("p t (c i) -> p c t i", i=4),
+            )
+            nc.scalar.copy(
+                out=wgrp[nm][:, CV:N, :].rearrange("p (c i) t -> p c t i", i=4),
+                in_=raw[nm][:, :, CV:N].rearrange("p t (c i) -> p c t i", i=4),
+            )
+
+        def quantise_w(nm):
+            wcodes[nm] = keep.tile([P, N], U32, name="wc_" + nm, align_bytes=64)
+            wscales[nm] = keep.tile([P, N], U8, name="ws_" + nm, align_bytes=64)
+            nc.vector.quantize_mx(
+                out=wcodes[nm][:].bitcast(E4X4),
+                scales=wscales[nm][:],
+                in_=wgrp[nm][:].rearrange("p c t -> p (c t)"),
+            )
+
+        xt = {}
+        unit_of = {}
+        ggrp, gcodes, gscales = {}, {}, {}
+
+        def transposes(b):
+            xt[b] = new_bank()
+            for j in range(2):
+                ci, loc = chunk_of[2 * b + j]
+                words = g_tiles[ci][:].bitcast(F32)
+                for u in range(2):
+                    nc.tensor.transpose(
+                        xt[b][1][:, (2 * j + u) * P : (2 * j + u + 1) * P],
+                        words[:, loc * 256 + u * P : loc * 256 + (u + 1) * P],
+                        ident[:],
+                    )
+
+        def copy_out(b, on_vector):
+            unit, half = unit_of[b]
+            if unit not in ggrp:
+                ggrp[unit] = ring.tile([P, 2048], BF16, name="gg%d" % unit, tag="gg%d" % (unit % GRP_BUFS), align_bytes=64)
+            dst = ggrp[unit][:, half * 1024 : (half + 1) * 1024].bitcast(F32).rearrange("p (j m u) -> p j m u", j=2, u=2)
+            src = xt[b][1][:].rearrange("p (j u m) -> p j m u", j=2, u=2)
+            if on_vector:
+                nc.vector.tensor_copy(out=dst, in_=src)
+            else:
+                nc.scalar.copy(out=dst, in_=src)
+            free_banks.append(xt[b][0])
+
+        def quantise_unit(unit, pairs):
+            gcodes[unit] = keep.tile([P, 256 * pairs], U32, name="gc%d" % unit, align_bytes=64)
+            gscales[unit] = keep.tile([P, 256 * pairs], U8, name="gs%d" % unit, align_bytes=64)
+            nc.vector.quantize_mx(
+                out=gcodes[unit][:].bitcast(E5X4),
+                scales=gscales[unit][:],
+                in_=ggrp[unit][:, 0 : 1024 * pairs],
+            )
+
+        acc = {}
+        asb = {}
+        stage = {}
+        store_of = []
+        for si, sz in enumerate(S_CHUNKS):
+            for j in range(sz):
+                store_of.append((si, j))
+
+        def matmuls(n):
+            unit, half = unit_of[n // 2]
+            c0 = (2 * half + n % 2) * P
+            for nm in ("w", "pg"):
+                acc[(n, nm)] = new_bank()
+                nc.tensor.matmul_mx(
+                    out=acc[(n, nm)][1][:],
+                    lhsT=gcodes[unit][:, c0 : c0 + P].bitcast(E5X4),
+                    lhsT_scale=gscales[unit][:, c0 : c0 + P],
+                    rhs=wcodes[nm][:].bitcast(E4X4),
+                    rhs_scale=wscales[nm][:],
+                    start=True,
+                    stop=True,
+                )
+
+        def combine(n):
+            asb[n] = ring.tile([P, N], F32, name="asb%d" % n, tag="asb%d" % (n % ASB_BUFS))
+            nc.scalar.copy(out=asb[n][:], in_=acc[(n, "w")][1][:])
+            free_banks.append(acc[(n, "w")][0])
+            si, j = store_of[n]
+            sz = S_CHUNKS[si]
+            if j == 0:
+                stage[si] = ring.tile([P, sz * N], F32, name="st%d" % si, tag="st%d" % (si % STAGE_BUFS))
+            nc.vector.scalar_tensor_tensor(
+                out=stage[si][:, j * N : (j + 1) * N],
+                in0=acc[(n, "pg")][1][:],
+                scalar=nlr[:, n : n + 1],
+                in1=asb[n][:],
+                op0=MULT,
+                op1=ADD,
+            )
+            free_banks.append(acc[(n, "pg")][0])
+            if j == sz - 1:
+                nc.sync.dma_start(out=out_rows[:, (n + 1 - sz) * N : (n + 1) * N], in_=stage[si][:])
+
+        groups = front_groups()
+        units = {}
+        unit_of[0] = (0, 0)
+        next_unit = 1
+        for gi, (b0, npairs, at, vsel) in enumerate(groups):
+            units[gi] = []
+            for k in range(0, npairs, 2):
+                w = min(2, npairs - k)
+                for h in range(w):
+                    unit_of[b0 + k + h] = (next_unit, h)
+                units[gi].append((next_unit, w))
+                next_unit += 1
+
+        nlr = keep.tile([P, NT], F32, name="nlr")
+        transposes(0)
+        regroup_w("w")
+        copy_out(0, False)
+        quantise_w("w")
+        regroup_w("pg")
+        nc.vector.tensor_scalar_mul(out=nlr[:], in0=lrb[:], scalar1=-1.0)
+        quantise_unit(0, 1)
+        quantise_w("pg")
+
+        for n in range(NT + 1):
+            if n < NT:
+                for b0, npairs, at, vsel in groups:
+                    if at == n:
+                        for b in range(b0, b0 + npairs):
+                            transposes(b)
+                matmuls(n)
+            m = n - 1
+            if m >= 0:
+                for gi, (b0, npairs, at, vsel) in enumerate(groups):
+                    if at == m:
+                        for k in range(npairs):
+                            copy_out(b0 + k, k == vsel)
+                        for unit, w in units[gi]:
+                            quantise_unit(unit, w)
+                combine(m)

@@ -29,7 +29,7 @@ CV = 336
 def front_groups():
     groups = [(1, 1, 0, None), (2, 2, 2, 1), (4, 4, 4, 2)]
     for j in range(2, 8):
-        groups.append((4 * j, 4, 8 * j - 2, 2))
+        groups.append((4 * j, 4, 8 * j - 4, 2))
     return groups
 
 

@@ -73,9 +73,9 @@ def tile_optimizedlinear_t_kernel(
             first = sum(G_CHUNKS[:ci])
             nc.sync.dma_start(out=g_tiles[ci][:], in_=g_rows[:, first * K : (first + G_CHUNKS[ci]) * K])
 
-        load_w("w", weight)
-        load_g(0)
         load_w("pg", prev_grad)
+        load_g(0)
+        load_w("w", weight)
         nc.sync.dma_start(out=lrb[:], in_=lr_rows)
         for ci in range(1, len(G_CHUNKS)):
             load_g(ci)
@@ -160,7 +160,7 @@ def tile_optimizedlinear_t_kernel(
         def matmuls(n):
             unit, half = unit_of[n // 2]
             c0 = (2 * half + n % 2) * P
-            for nm in ("w", "pg"):
+            for nm in ("pg", "w"):
                 acc[(n, nm)] = new_bank()
                 nc.tensor.matmul_mx(
                     out=acc[(n, nm)][1][:],
@@ -173,18 +173,17 @@ def tile_optimizedlinear_t_kernel(
                 )
 
         def combine(n):
-            asb[n] = ring.tile([P, N], F32, name="asb%d" % n, tag="asb%d" % (n % ASB_BUFS))
-            nc.scalar.copy(out=asb[n][:], in_=acc[(n, "w")][1][:])
-            free_banks.append(acc[(n, "w")][0])
             si, j = store_of[n]
             sz = S_CHUNKS[si]
             if j == 0:
                 stage[si] = ring.tile([P, sz * N], F32, name="st%d" % si, tag="st%d" % (si % STAGE_BUFS))
+            nc.scalar.copy(out=stage[si][:, j * N : (j + 1) * N], in_=acc[(n, "w")][1][:])
+            free_banks.append(acc[(n, "w")][0])
             nc.vector.scalar_tensor_tensor(
                 out=stage[si][:, j * N : (j + 1) * N],
                 in0=acc[(n, "pg")][1][:],
                 scalar=nlr[:, n : n + 1],
-                in1=asb[n][:],
+                in1=stage[si][:, j * N : (j + 1) * N],
                 op0=MULT,
                 op1=ADD,
             )
@@ -207,13 +206,13 @@ def tile_optimizedlinear_t_kernel(
 
         nlr = keep.tile([P, NT], F32, name="nlr")
         transposes(0)
-        regroup_w("w")
-        copy_out(0, False)
-        quantise_w("w")
         regroup_w("pg")
+        copy_out(0, False)
+        quantise_w("pg")
+        regroup_w("w")
         nc.vector.tensor_scalar_mul(out=nlr[:], in0=lrb[:], scalar1=-1.0)
         quantise_unit(0, 1)
-        quantise_w("pg")
+        quantise_w("w")
 
         for n in range(NT + 1):
             if n < NT:

@@ -27,7 +27,7 @@ CV = 336
 
 
 def front_groups():
-    groups = [(1, 1, 0, None), (2, 2, 2, 1), (4, 4, 4, 2)]
+    groups = [(1, 1, 0, None), (2, 2, 0, 1), (4, 4, 4, 2)]
     for j in range(2, 8):
         groups.append((4 * j, 4, 8 * j - 4, 2))
     return groups
@@ -73,12 +73,13 @@ def tile_optimizedlinear_t_kernel(
             first = sum(G_CHUNKS[:ci])
             nc.sync.dma_start(out=g_tiles[ci][:], in_=g_rows[:, first * K : (first + G_CHUNKS[ci]) * K])
 
-        load_w("pg", prev_grad)
-        load_g(0)
         load_w("w", weight)
-        nc.sync.dma_start(out=lrb[:], in_=lr_rows)
+        load_g(0)
+        load_w("pg", prev_grad)
         for ci in range(1, len(G_CHUNKS)):
             load_g(ci)
+            if ci == 2:
+                nc.sync.dma_start(out=lrb[:], in_=lr_rows)
 
         free_banks = list(range(8))
         head = [0]
@@ -160,7 +161,7 @@ def tile_optimizedlinear_t_kernel(
         def matmuls(n):
             unit, half = unit_of[n // 2]
             c0 = (2 * half + n % 2) * P
-            for nm in ("pg", "w"):
+            for nm in ("w", "pg"):
                 acc[(n, nm)] = new_bank()
                 nc.tensor.matmul_mx(
                     out=acc[(n, nm)][1][:],
@@ -173,17 +174,18 @@ def tile_optimizedlinear_t_kernel(
                 )
 
         def combine(n):
+            asb[n] = ring.tile([P, N], F32, name="asb%d" % n, tag="asb%d" % (n % ASB_BUFS))
+            nc.scalar.copy(out=asb[n][:], in_=acc[(n, "w")][1][:])
+            free_banks.append(acc[(n, "w")][0])
             si, j = store_of[n]
             sz = S_CHUNKS[si]
             if j == 0:
                 stage[si] = ring.tile([P, sz * N], F32, name="st%d" % si, tag="st%d" % (si % STAGE_BUFS))
-            nc.scalar.copy(out=stage[si][:, j * N : (j + 1) * N], in_=acc[(n, "w")][1][:])
-            free_banks.append(acc[(n, "w")][0])
             nc.vector.scalar_tensor_tensor(
                 out=stage[si][:, j * N : (j + 1) * N],
                 in0=acc[(n, "pg")][1][:],
                 scalar=nlr[:, n : n + 1],
-                in1=stage[si][:, j * N : (j + 1) * N],
+                in1=asb[n][:],
                 op0=MULT,
                 op1=ADD,
             )
@@ -206,13 +208,13 @@ def tile_optimizedlinear_t_kernel(
 
         nlr = keep.tile([P, NT], F32, name="nlr")
         transposes(0)
-        regroup_w("pg")
-        copy_out(0, False)
-        quantise_w("pg")
         regroup_w("w")
-        nc.vector.tensor_scalar_mul(out=nlr[:], in0=lrb[:], scalar1=-1.0)
-        quantise_unit(0, 1)
+        copy_out(0, False)
         quantise_w("w")
+        regroup_w("pg")
+        quantise_unit(0, 1)
+        quantise_w("pg")
+        nc.vector.tensor_scalar_mul(out=nlr[:], in0=lrb[:], scalar1=-1.0)
 
         for n in range(NT + 1):
             if n < NT:

@@ -24,6 +24,7 @@ STAGE_BUFS = 8
 ASB_BUFS = 4
 GRP_BUFS = 4
 CV = 336
+WARM_FIRST, WARM_W, WARM_PG = 6, 2, 3
 
 
 def front_groups():
@@ -49,6 +50,8 @@ def tile_optimizedlinear_t_kernel(
 
         ident = keep.tile([P, P], F32, name="ident")
         make_identity(nc, ident[:])
+        warm = keep.tile([P, N], BF16, name="warm")
+        nc.vector.memset(warm[:], 0.0)
 
         raw = {}
         for nm in ("w", "pg"):
@@ -90,6 +93,12 @@ def tile_optimizedlinear_t_kernel(
             head[0] += 1
             serial[0] += 1
             return k, psum.tile([P, 512], F32, name="ps%d" % serial[0], tag="bank%d" % k)
+
+        dummy_bank = new_bank()
+
+        def dummies(count, lhsT, rhs):
+            for i in range(count):
+                nc.tensor.matmul(dummy_bank[1][:], lhsT=lhsT, rhs=rhs, start=True, stop=True)
 
         wgrp, wcodes, wscales = {}, {}, {}
 
@@ -207,7 +216,11 @@ def tile_optimizedlinear_t_kernel(
                 next_unit += 1
 
         nlr = keep.tile([P, NT], F32, name="nlr")
+        dummies(WARM_FIRST, warm[:, 0:P], warm[:])
+        dummies(WARM_W, raw["w"][:, 0, 0:P], raw["w"][:, 1, :])
         transposes(0)
+        dummies(WARM_PG, raw["pg"][:, 0, 0:P], raw["pg"][:, 1, :])
+        free_banks.append(dummy_bank[0])
         regroup_w("w")
         copy_out(0, False)
         quantise_w("w")

@@ -9,8 +9,8 @@ U32 = mybir.dt.uint32
 U8 = mybir.dt.uint8
 E4X4 = mybir.dt.float8_e4m3fn_x4
 E5X4 = mybir.dt.float8_e5m2_x4
-MULT = mybir.AluOpType.mult
 ADD = mybir.AluOpType.add
+COPY = mybir.ActivationFunctionType.Copy
 
 P = 128
 B, K, N = 8192, 512, 512
@@ -76,9 +76,9 @@ def tile_optimizedlinear_t_kernel(
             first = sum(G_CHUNKS[:ci])
             nc.sync.dma_start(out=g_tiles[ci][:], in_=g_rows[:, first * K : (first + G_CHUNKS[ci]) * K])
 
-        load_w("w", weight)
-        load_g(0)
         load_w("pg", prev_grad)
+        load_g(0)
+        load_w("w", weight)
         for ci in range(1, len(G_CHUNKS)):
             load_g(ci)
             if ci == 2:
@@ -170,7 +170,7 @@ def tile_optimizedlinear_t_kernel(
         def matmuls(n):
             unit, half = unit_of[n // 2]
             c0 = (2 * half + n % 2) * P
-            for nm in ("w", "pg"):
+            for nm in ("pg", "w"):
                 acc[(n, nm)] = new_bank()
                 nc.tensor.matmul_mx(
                     out=acc[(n, nm)][1][:],
@@ -184,21 +184,19 @@ def tile_optimizedlinear_t_kernel(
 
         def combine(n):
             asb[n] = ring.tile([P, N], F32, name="asb%d" % n, tag="asb%d" % (n % ASB_BUFS))
-            nc.scalar.copy(out=asb[n][:], in_=acc[(n, "w")][1][:])
-            free_banks.append(acc[(n, "w")][0])
+            nc.scalar.activation(out=asb[n][:], in_=acc[(n, "pg")][1][:], func=COPY, scale=nlr[:, n : n + 1])
+            free_banks.append(acc[(n, "pg")][0])
             si, j = store_of[n]
             sz = S_CHUNKS[si]
             if j == 0:
                 stage[si] = ring.tile([P, sz * N], F32, name="st%d" % si, tag="st%d" % (si % STAGE_BUFS))
-            nc.vector.scalar_tensor_tensor(
+            nc.vector.tensor_tensor(
                 out=stage[si][:, j * N : (j + 1) * N],
-                in0=acc[(n, "pg")][1][:],
-                scalar=nlr[:, n : n + 1],
+                in0=acc[(n, "w")][1][:],
                 in1=asb[n][:],
-                op0=MULT,
-                op1=ADD,
+                op=ADD,
             )
-            free_banks.append(acc[(n, "pg")][0])
+            free_banks.append(acc[(n, "w")][0])
             if j == sz - 1:
                 nc.sync.dma_start(out=out_rows[:, (n + 1 - sz) * N : (n + 1) * N], in_=stage[si][:])
 
@@ -217,16 +215,16 @@ def tile_optimizedlinear_t_kernel(
 
         nlr = keep.tile([P, NT], F32, name="nlr")
         dummies(WARM_FIRST, warm[:, 0:P], warm[:])
-        dummies(WARM_W, raw["w"][:, 0, 0:P], raw["w"][:, 1, :])
+        dummies(WARM_W, raw["pg"][:, 0, 0:P], raw["pg"][:, 1, :])
         transposes(0)
-        dummies(WARM_PG, raw["pg"][:, 0, 0:P], raw["pg"][:, 1, :])
+        dummies(WARM_PG, raw["w"][:, 0, 0:P], raw["w"][:, 1, :])
         free_banks.append(dummy_bank[0])
-        regroup_w("w")
-        copy_out(0, False)
-        quantise_w("w")
         regroup_w("pg")
-        quantise_unit(0, 1)
+        copy_out(0, False)
         quantise_w("pg")
+        regroup_w("w")
+        quantise_unit(0, 1)
+        quantise_w("w")
         nc.vector.tensor_scalar_mul(out=nlr[:], in0=lrb[:], scalar1=-1.0)
 
         for n in range(NT + 1):

from contextlib import ExitStack

import concourse.mybir as mybir
from concourse.masks import make_identity

F32 = mybir.dt.float32
BF16 = mybir.dt.bfloat16
U32 = mybir.dt.uint32
U8 = mybir.dt.uint8
E4X4 = mybir.dt.float8_e4m3fn_x4
E5X4 = mybir.dt.float8_e5m2_x4
ADD = mybir.AluOpType.add
COPY = mybir.ActivationFunctionType.Copy

P = 128
B, K, N = 8192, 512, 512
NT = B // P
FLOPS = 2 * 2 * B * K * N
BYTES = B * K * 2 + 2 * K * N * 2 + B * 2 + B * N * 4

G_CHUNKS = [2, 2, 4, 8, 16, 16, 16]
S_CHUNKS = [4] * 13 + [2, 2, 2, 2, 1, 1, 1, 1]
STAGE_BUFS = 8
ASB_BUFS = 4
GRP_BUFS = 4
CV = 336
WARM_FIRST, WARM_W, WARM_PG = 6, 2, 3


def front_groups():
    groups = [(1, 1, 0, None), (2, 2, 0, 1), (4, 4, 4, 2)]
    for j in range(2, 8):
        groups.append((4 * j, 4, 8 * j - 4, 2))
    return groups


def tile_optimizedlinear_t_kernel(
    tc, input_data, weight, bias, prev_grad, prev_bias_grad, lr_samples, grad_out, out
):
    nc = tc.nc
    g_rows = grad_out.rearrange("(p n) k -> p (n k)", n=NT)
    out_rows = out.rearrange("(p n) i -> p (n i)", n=NT)
    lr_rows = lr_samples.rearrange("(p n) -> p n", n=NT)

    with ExitStack() as ctx:
        keep = ctx.enter_context(tc.tile_pool(name="keep", bufs=1))
        ring = ctx.enter_context(tc.tile_pool(name="ring", bufs=1))
        psum = ctx.enter_context(tc.psum_pool(name="psum", bufs=1))
        ctx.enter_context(tc.manual_schedule())

        ident = keep.tile([P, P], F32, name="ident")
        make_identity(nc, ident[:])
        warm = keep.tile([P, N], BF16, name="warm")
        nc.vector.memset(warm[:], 0.0)

        raw = {}
        for nm in ("w", "pg"):
            raw[nm] = keep.tile([P, 4, N], BF16, name="raw_" + nm)
        lrb = keep.tile([P, NT], BF16, name="lrb")
        g_tiles = []
        chunk_of = []
        t0 = 0
        for ci, sz in enumerate(G_CHUNKS):
            g_tiles.append(keep.tile([P, sz * K], BF16, name="g%d" % ci))
            for j in range(sz):
                chunk_of.append((ci, j))
            t0 += sz

        def load_w(nm, src):
            nc.sync.dma_start(
                out=raw[nm][:].rearrange("p (u e) c -> p u (e c)", u=2),
                in_=src.rearrange("(u q e) c -> q u (e c)", u=2, e=2),
            )

        def load_g(ci):
            first = sum(G_CHUNKS[:ci])
            nc.sync.dma_start(out=g_tiles[ci][:], in_=g_rows[:, first * K : (first + G_CHUNKS[ci]) * K])

        load_w("pg", prev_grad)
        load_g(0)
        load_w("w", weight)
        for ci in range(1, len(G_CHUNKS)):
            load_g(ci)
            if ci == 2:
                nc.sync.dma_start(out=lrb[:], in_=lr_rows)

        free_banks = list(range(8))
        head = [0]
        serial = [0]

        def new_bank():
            k = free_banks[head[0]]
            head[0] += 1
            serial[0] += 1
            return k, psum.tile([P, 512], F32, name="ps%d" % serial[0], tag="bank%d" % k)

        dummy_bank = new_bank()

        def dummies(count, lhsT, rhs):
            for i in range(count):
                nc.tensor.matmul(dummy_bank[1][:], lhsT=lhsT, rhs=rhs, start=True, stop=True)

        wgrp, wcodes, wscales = {}, {}, {}

        def regroup_w(nm):
            wgrp[nm] = keep.tile([P, N, 4], BF16, name="grp_" + nm, align_bytes=64)
            nc.vector.tensor_copy(
                out=wgrp[nm][:, 0:CV, :].rearrange("p (c i) t -> p c t i", i=4),
                in_=raw[nm][:, :, 0:CV].rearrange("p t (c i) -> p c t i", i=4),
            )
            nc.scalar.copy(
                out=wgrp[nm][:, CV:N, :].rearrange("p (c i) t -> p c t i", i=4),
                in_=raw[nm][:, :, CV:N].rearrange("p t (c i) -> p c t i", i=4),
            )

        def quantise_w(nm):
            wcodes[nm] = keep.tile([P, N], U32, name="wc_" + nm, align_bytes=64)
            wscales[nm] = keep.tile([P, N], U8, name="ws_" + nm, align_bytes=64)
            nc.vector.quantize_mx(
                out=wcodes[nm][:].bitcast(E4X4),
                scales=wscales[nm][:],
                in_=wgrp[nm][:].rearrange("p c t -> p (c t)"),
            )

        xt = {}
        unit_of = {}
        ggrp, gcodes, gscales = {}, {}, {}

        def transposes(b):
            xt[b] = new_bank()
            for j in range(2):
                ci, loc = chunk_of[2 * b + j]
                words = g_tiles[ci][:].bitcast(F32)
                for u in range(2):
                    nc.tensor.transpose(
                        xt[b][1][:, (2 * j + u) * P : (2 * j + u + 1) * P],
                        words[:, loc * 256 + u * P : loc * 256 + (u + 1) * P],
                        ident[:],
                    )

        def copy_out(b, on_vector):
            unit, half = unit_of[b]
            if unit not in ggrp:
                ggrp[unit] = ring.tile([P, 2048], BF16, name="gg%d" % unit, tag="gg%d" % (unit % GRP_BUFS), align_bytes=64)
            dst = ggrp[unit][:, half * 1024 : (half + 1) * 1024].bitcast(F32).rearrange("p (j m u) -> p j m u", j=2, u=2)
            src = xt[b][1][:].rearrange("p (j u m) -> p j m u", j=2, u=2)
            if on_vector:
                nc.vector.tensor_copy(out=dst, in_=src)
            else:
                nc.scalar.copy(out=dst, in_=src)
            free_banks.append(xt[b][0])

        def quantise_unit(unit, pairs):
            gcodes[unit] = keep.tile([P, 256 * pairs], U32, name="gc%d" % unit, align_bytes=64)
            gscales[unit] = keep.tile([P, 256 * pairs], U8, name="gs%d" % unit, align_bytes=64)
            nc.vector.quantize_mx(
                out=gcodes[unit][:].bitcast(E5X4),
                scales=gscales[unit][:],
                in_=ggrp[unit][:, 0 : 1024 * pairs],
            )

        acc = {}
        asb = {}
        stage = {}
        store_of = []
        for si, sz in enumerate(S_CHUNKS):
            for j in range(sz):
                store_of.append((si, j))

        def matmuls(n):
            unit, half = unit_of[n // 2]
            c0 = (2 * half + n % 2) * P
            for nm in ("pg", "w"):
                acc[(n, nm)] = new_bank()
                nc.tensor.matmul_mx(
                    out=acc[(n, nm)][1][:],
                    lhsT=gcodes[unit][:, c0 : c0 + P].bitcast(E5X4),
                    lhsT_scale=gscales[unit][:, c0 : c0 + P],
                    rhs=wcodes[nm][:].bitcast(E4X4),
                    rhs_scale=wscales[nm][:],
                    start=True,
                    stop=True,
                )

        def combine(n):
            asb[n] = ring.tile([P, N], F32, name="asb%d" % n, tag="asb%d" % (n % ASB_BUFS))
            nc.scalar.activation(out=asb[n][:], in_=acc[(n, "pg")][1][:], func=COPY, scale=nlr[:, n : n + 1])
            free_banks.append(acc[(n, "pg")][0])
            si, j = store_of[n]
            sz = S_CHUNKS[si]
            if j == 0:
                stage[si] = ring.tile([P, sz * N], F32, name="st%d" % si, tag="st%d" % (si % STAGE_BUFS))
            nc.vector.tensor_tensor(
                out=stage[si][:, j * N : (j + 1) * N],
                in0=acc[(n, "w")][1][:],
                in1=asb[n][:],
                op=ADD,
            )
            free_banks.append(acc[(n, "w")][0])
            if j == sz - 1:
                nc.sync.dma_start(out=out_rows[:, (n + 1 - sz) * N : (n + 1) * N], in_=stage[si][:])

        groups = front_groups()
        units = {}
        unit_of[0] = (0, 0)
        next_unit = 1
        for gi, (b0, npairs, at, vsel) in enumerate(groups):
            units[gi] = []
            for k in range(0, npairs, 2):
                w = min(2, npairs - k)
                for h in range(w):
                    unit_of[b0 + k + h] = (next_unit, h)
                units[gi].append((next_unit, w))
                next_unit += 1

        nlr = keep.tile([P, NT], F32, name="nlr")
        dummies(WARM_FIRST, warm[:, 0:P], warm[:])
        dummies(WARM_W, raw["pg"][:, 0, 0:P], raw["pg"][:, 1, :])
        transposes(0)
        dummies(WARM_PG, raw["w"][:, 0, 0:P], raw["w"][:, 1, :])
        free_banks.append(dummy_bank[0])
        regroup_w("pg")
        copy_out(0, False)
        quantise_w("pg")
        regroup_w("w")
        quantise_unit(0, 1)
        quantise_w("w")
        nc.vector.tensor_scalar_mul(out=nlr[:], in0=lrb[:], scalar1=-1.0)

        for n in range(NT + 1):
            if n < NT:
                for b0, npairs, at, vsel in groups:
                    if at == n:
                        for b in range(b0, b0 + npairs):
                            transposes(b)
                matmuls(n)
            m = n - 1
            if m >= 0:
                for gi, (b0, npairs, at, vsel) in enumerate(groups):
                    if at == m:
                        for k in range(npairs):
                            copy_out(b0 + k, k == vsel)
                        for unit, w in units[gi]:
                            quantise_unit(unit, w)
                combine(m)
